import numpy as np
import ml_dtypes


def mxq(x, axis, fmt="e4m3"):
    dtype, down = {"e4m3": (ml_dtypes.float8_e4m3fn, 7), "e5m2": (ml_dtypes.float8_e5m2, 14)}[fmt]
    v = np.moveaxis(np.asarray(x, np.float32).astype(ml_dtypes.bfloat16).astype(np.float64), axis, -1)
    blocks = v.reshape(v.shape[:-1] + (-1, 32))
    amax = np.abs(blocks).max(-1, keepdims=True)
    byte = np.maximum(np.where(amax > 0, np.frexp(amax)[1] - 1 + 127, 0) - down, 1)
    scale = np.exp2(byte - 127.0)
    codes = (blocks / scale).astype(np.float32).astype(dtype).astype(np.float64)
    return np.moveaxis((codes * scale).reshape(v.shape), -1, axis)


WIDE = False


def mx_kscale(k):
    if not WIDE:
        return np.ones(k)
    levels = np.array([10, -10, 5, -5, 0])
    a = np.random.permutation(np.resize(levels, k // 512 * 4)).reshape(k // 512, 4)
    idx = np.arange(k)
    return np.exp2(a[idx // 512, idx % 128 // 32])


BF16 = ml_dtypes.bfloat16


def bf(x):
    return np.asarray(x, np.float32).astype(BF16)


def f64(x):
    return np.asarray(x).astype(np.float64)


B, S, HID, NH, HD, RD, RATIO = 1, 2048, 1024, 8, 128, 64, 4
THETA = 10000.0
HALF = RD // 2


def rope_tables(positions):
    inv_freq = 1.0 / THETA ** (np.arange(HALF) / HALF)
    ang = positions[:, None] * inv_freq[None, :]
    return np.cos(ang), np.sin(ang)


def rope_interleaved(x, cos, sin):
    nope, rope = x[..., :-RD], x[..., -RD:]
    pr = rope.reshape(rope.shape[:-1] + (HALF, 2))
    a, b = pr[..., 0], pr[..., 1]
    new = np.stack([a * cos - b * sin, a * sin + b * cos], axis=-1).reshape(rope.shape)
    return np.concatenate([nope, new], axis=-1)


def setup_inputs():
    s = mx_kscale(HID)
    return {"hidden": bf(np.random.standard_normal((B, S, HID)) * s),
            "wq": bf(np.random.standard_normal((HID, NH * HD)) / np.sqrt(HID) / s[:, None])}


def reference(hidden, wq):
    q = mxq(f64(hidden), 2, "e4m3") @ mxq(f64(wq), 0, "e4m3")
    q = q.reshape(B, S, NH, HD).transpose(0, 2, 1, 3)
    cq, sq = rope_tables(np.arange(S))
    return rope_interleaved(q, cq, sq)

@@ -1,0 +1,219 @@
+import math
+from contextlib import ExitStack
+
+import concourse.mybir as mybir
+from concourse.masks import make_identity
+
+F32 = mybir.dt.float32
+BF16 = mybir.dt.bfloat16
+I32 = mybir.dt.int32
+U32 = mybir.dt.uint32
+U8 = mybir.dt.uint8
+FP8X4 = mybir.dt.float8_e4m3fn_x4
+ALU = mybir.AluOpType
+ACT = mybir.ActivationFunctionType
+
+P = 128
+TOKENS = 2048
+HIDDEN = 1024
+HEADS = 8
+HEAD_DIM = 128
+PAIRS = 32
+PLAIN = HEAD_DIM - 2 * PAIRS
+THETA = 10000.0
+
+PACK = 4
+HALVES = 2
+K_PASS = P * PACK
+PASSES = HIDDEN // K_PASS
+BANK = 512
+
+TILES = TOKENS // P
+GROUP = 2
+GROUPS = TILES // GROUP
+
+ROTATED = 0
+COPIED = 1
+
+HIGH_WORD_GRID = 2.0**15
+
+FLOPS = 2 * TOKENS * HIDDEN * HEADS * HEAD_DIM
+
+
+def build_rotation_table(nc, pool, table):
+    warm = pool.tile([P, 1], F32)
+    nc.vector.memset(warm[:], 0.0)
+    nc.scalar.activation(out=warm[:], in_=warm[:], func=ACT.Sin)
+
+    token_int = pool.tile([P, TILES], I32)
+    nc.gpsimd.iota(token_int[:], pattern=[[1, TILES]], base=0, channel_multiplier=TILES)
+    token = pool.tile([P, TILES], F32)
+    nc.vector.tensor_copy(out=token[:], in_=token_int[:])
+
+    turns_high = pool.tile([P, TILES, PAIRS], F32)
+    turns_low = pool.tile([P, TILES, PAIRS], F32)
+    for j in range(PAIRS):
+        frequency = THETA ** (-j / PAIRS) / (2.0 * math.pi)
+        high_word = round(frequency * HIGH_WORD_GRID) / HIGH_WORD_GRID
+        nc.vector.tensor_scalar(
+            out=turns_high[:, :, j], in0=token[:], scalar1=high_word, scalar2=None, op0=ALU.mult
+        )
+        nc.scalar.activation(
+            out=turns_low[:, :, j], in_=token[:], func=ACT.Copy, scale=frequency - high_word
+        )
+
+    turns = pool.tile([P, TILES, PAIRS], F32)
+    nc.vector.tensor_tensor(out=turns[:], in0=turns_high[:], in1=turns_low[:], op=ALU.add)
+    whole = pool.tile([P, TILES, PAIRS], I32)
+    nc.vector.tensor_copy(out=whole[:], in_=turns[:])
+    high_rest = pool.tile([P, TILES, PAIRS], F32)
+    nc.vector.tensor_tensor(out=high_rest[:], in0=turns_high[:], in1=whole[:], op=ALU.subtract)
+    fraction = pool.tile([P, TILES, PAIRS], F32)
+    nc.vector.tensor_tensor(out=fraction[:], in0=high_rest[:], in1=turns_low[:], op=ALU.add)
+
+    minus_abs = pool.tile([P, TILES, PAIRS], F32)
+    nc.vector.scalar_tensor_tensor(
+        out=minus_abs[:], in0=fraction[:], scalar=-1.0, in1=fraction[:], op0=ALU.mult, op1=ALU.min
+    )
+    quarter_less_abs = pool.tile([P, TILES, PAIRS], F32)
+    nc.vector.tensor_scalar(
+        out=quarter_less_abs[:], in0=minus_abs[:], scalar1=0.25, scalar2=None, op0=ALU.add
+    )
+
+    turn = 2.0 * math.pi
+    nc.scalar.activation(out=table[:, :, 0, 0, :], in_=quarter_less_abs[:], func=ACT.Sin, scale=turn)
+    nc.scalar.activation(out=table[:, :, 0, 1, :], in_=fraction[:], func=ACT.Sin, scale=-turn)
+    nc.scalar.activation(out=table[:, :, 1, 0, :], in_=fraction[:], func=ACT.Sin, scale=turn)
+    nc.scalar.activation(out=table[:, :, 1, 1, :], in_=quarter_less_abs[:], func=ACT.Sin, scale=turn)
+
+
+def tile_deepseekv4attention_pb_kernel(tc, hidden, wq, out):
+    nc = tc.nc
+    with ExitStack() as ctx:
+        keep = ctx.enter_context(tc.tile_pool(name="keep", bufs=1))
+        w_stage = ctx.enter_context(tc.tile_pool(name="w_stage", bufs=2))
+        h_stage = ctx.enter_context(tc.tile_pool(name="h_stage", bufs=3))
+        work = ctx.enter_context(tc.tile_pool(name="work", bufs=3))
+        flipped_banks = ctx.enter_context(tc.psum_pool(name="flipped_banks", bufs=2))
+        rotated_banks = ctx.enter_context(tc.psum_pool(name="rotated_banks", bufs=3))
+        copied_banks = ctx.enter_context(tc.psum_pool(name="copied_banks", bufs=3))
+
+        hidden_groups = hidden[0].rearrange("(p n x) k -> n p (x k)", n=GROUPS, x=GROUP)
+        out_groups = out[0].rearrange("h (p n x) d -> n p h (x d)", n=GROUPS, x=GROUP)
+
+        h_raw = []
+        for n in range(GROUPS):
+            h_raw.append(keep.tile([P, GROUP * HIDDEN], BF16, name="h_raw%d" % n))
+        w_raw = keep.tile([P, PASSES, PACK, HEADS * HEAD_DIM], BF16)
+
+        nc.sync.dma_start(out=h_raw[0][:], in_=hidden_groups[0])
+        for g in range(PASSES):
+            nc.sync.dma_start(
+                out=w_raw[:, g].rearrange("q (u e) n -> q u (e n)", u=HALVES),
+                in_=wq[g * K_PASS : (g + 1) * K_PASS, :].rearrange(
+                    "(u q e) n -> q u (e n)", u=HALVES, q=P
+                ),
+            )
+        for n in range(1, GROUPS):
+            nc.sync.dma_start(out=h_raw[n][:], in_=hidden_groups[n])
+
+        table = keep.tile([P, TILES, 2, 2, PAIRS], F32)
+        build_rotation_table(nc, keep, table)
+
+        identity = keep.tile([P, P], F32)
+        make_identity(nc, identity[:])
+
+        def quantise_hidden(n):
+            raw_words = h_raw[n][:].bitcast(F32).rearrange("m (x w) -> m x w", x=GROUP)
+            grouped = h_stage.tile([P, GROUP * PASSES * P * PACK], BF16, align_bytes=64)
+            grouped_words = grouped[:].bitcast(F32).rearrange(
+                "q (x g m u) -> q x g m u", x=GROUP, g=PASSES, u=HALVES
+            )
+            for x in range(GROUP):
+                flipped = flipped_banks.tile([P, PASSES * HALVES, P], F32)
+                for c in range(PASSES * HALVES):
+                    nc.tensor.transpose(
+                        flipped[:, c, :], raw_words[:, x, c * P : (c + 1) * P], identity[:]
+                    )
+                nc.scalar.copy(
+                    out=grouped_words[:, x],
+                    in_=flipped[:].rearrange("q (g u) m -> q g m u", u=HALVES),
+                )
+            codes = h_stage.tile([P, GROUP * PASSES * P], U32, align_bytes=64)
+            scales = h_stage.tile([P, GROUP * PASSES * P], U8, align_bytes=64)
+            nc.vector.quantize_mx(out=codes[:].bitcast(FP8X4), scales=scales[:], in_=grouped[:])
+            return codes, scales
+
+        w_codes = keep.tile([P, PASSES, 2, BANK], U32, align_bytes=64)
+        w_scales = keep.tile([P, PASSES, 2, BANK], U8, align_bytes=64)
+
+        def quantise_wq(g):
+            by_feature = w_raw[:, g].rearrange("q t (h s c) -> q s h c t", h=HEADS, s=2)
+
+            rotated = w_stage.tile([P, BANK * PACK], BF16, align_bytes=64)
+            rotated_out = rotated[:].rearrange("q (r h j t) -> q r h j t", r=2, h=HEADS, t=PACK)
+            rotated_in = by_feature[:, 1].rearrange("q h (j r) t -> q r h j t", r=2)
+            for r in range(2):
+                nc.vector.tensor_copy(out=rotated_out[:, r], in_=rotated_in[:, r])
+
+            copied = w_stage.tile([P, BANK * PACK], BF16, align_bytes=64)
+            nc.scalar.copy(
+                out=copied[:].rearrange("q (h c t) -> q h c t", h=HEADS, t=PACK),
+                in_=by_feature[:, 0],
+            )
+
+            for part, grouped in ((ROTATED, rotated), (COPIED, copied)):
+                nc.vector.quantize_mx(
+                    out=w_codes[:, g, part, :].bitcast(FP8X4),
+                    scales=w_scales[:, g, part, :],
+                    in_=grouped[:],
+                )
+
+        def project_and_rotate(n, codes, scales):
+            result = work.tile([P, HEADS, GROUP, HEAD_DIM], F32)
+            for x in range(GROUP):
+                rotated_acc = rotated_banks.tile([P, BANK], F32)
+                copied_acc = copied_banks.tile([P, BANK], F32)
+                for part, acc in ((ROTATED, rotated_acc), (COPIED, copied_acc)):
+                    for g in range(PASSES):
+                        tokens = slice((x * PASSES + g) * P, (x * PASSES + g + 1) * P)
+                        nc.tensor.matmul_mx(
+                            out=acc[:],
+                            lhsT=codes[:, tokens].bitcast(FP8X4),
+                            lhsT_scale=scales[:, tokens],
+                            rhs=w_codes[:, g, part, :].bitcast(FP8X4),
+                            rhs_scale=w_scales[:, g, part, :],
+                            start=(g == 0),
+                            stop=(g == PASSES - 1),
+                        )
+
+                shape = [P, 2, 2, HEADS, PAIRS]
+                products = work.tile(shape, F32)
+                nc.vector.tensor_tensor(
+                    out=products[:],
+                    in0=rotated_acc[:]
+                    .rearrange("p (r h j) -> p r h j", r=2, h=HEADS)
+                    .unsqueeze(1)
+                    .to_broadcast(shape),
+                    in1=table[:, n * GROUP + x].unsqueeze(3).to_broadcast(shape),
+                    op=ALU.mult,
+                )
+                nc.vector.tensor_tensor(
+                    out=result[:, :, x, PLAIN:].rearrange("p h (j s) -> p h j s", s=2),
+                    in0=products[:, :, 0].rearrange("p s h j -> p h j s"),
+                    in1=products[:, :, 1].rearrange("p s h j -> p h j s"),
+                    op=ALU.add,
+                )
+                nc.scalar.copy(
+                    out=result[:, :, x, :PLAIN],
+                    in_=copied_acc[:].rearrange("p (h c) -> p h c", h=HEADS),
+                )
+            nc.sync.dma_start(out=out_groups[n], in_=result[:].rearrange("p h x d -> p h (x d)"))
+
+        quantised = quantise_hidden(0)
+        for g in range(PASSES):
+            quantise_wq(g)
+        for n in range(GROUPS):
+            following = quantise_hidden(n + 1) if n + 1 < GROUPS else None
+            project_and_rotate(n, quantised[0], quantised[1])
+            quantised = following

@@ -198,7 +198,7 @@ def tile_deepseekv4attention_pb_kernel(tc, hidden, wq, out):
                     in1=table[:, n * GROUP + x].unsqueeze(3).to_broadcast(shape),
                     op=ALU.mult,
                 )
-                nc.vector.tensor_tensor(
+                nc.gpsimd.tensor_tensor(
                     out=result[:, :, x, PLAIN:].rearrange("p h (j s) -> p h j s", s=2),
                     in0=products[:, :, 0].rearrange("p s h j -> p h j s"),
                     in1=products[:, :, 1].rearrange("p s h j -> p h j s"),

@@ -31,60 +31,12 @@ BANK = 512
 TILES = TOKENS // P
 GROUP = 2
 GROUPS = TILES // GROUP
+AHEAD = 2
 
 ROTATED = 0
 COPIED = 1
 
-HIGH_WORD_GRID = 2.0**15
-
 FLOPS = 2 * TOKENS * HIDDEN * HEADS * HEAD_DIM
-
-
-def build_rotation_table(nc, pool, table):
-    warm = pool.tile([P, 1], F32)
-    nc.vector.memset(warm[:], 0.0)
-    nc.scalar.activation(out=warm[:], in_=warm[:], func=ACT.Sin)
-
-    token_int = pool.tile([P, TILES], I32)
-    nc.gpsimd.iota(token_int[:], pattern=[[1, TILES]], base=0, channel_multiplier=TILES)
-    token = pool.tile([P, TILES], F32)
-    nc.vector.tensor_copy(out=token[:], in_=token_int[:])
-
-    turns_high = pool.tile([P, TILES, PAIRS], F32)
-    turns_low = pool.tile([P, TILES, PAIRS], F32)
-    for j in range(PAIRS):
-        frequency = THETA ** (-j / PAIRS) / (2.0 * math.pi)
-        high_word = round(frequency * HIGH_WORD_GRID) / HIGH_WORD_GRID
-        nc.vector.tensor_scalar(
-            out=turns_high[:, :, j], in0=token[:], scalar1=high_word, scalar2=None, op0=ALU.mult
-        )
-        nc.scalar.activation(
-            out=turns_low[:, :, j], in_=token[:], func=ACT.Copy, scale=frequency - high_word
-        )
-
-    turns = pool.tile([P, TILES, PAIRS], F32)
-    nc.vector.tensor_tensor(out=turns[:], in0=turns_high[:], in1=turns_low[:], op=ALU.add)
-    whole = pool.tile([P, TILES, PAIRS], I32)
-    nc.vector.tensor_copy(out=whole[:], in_=turns[:])
-    high_rest = pool.tile([P, TILES, PAIRS], F32)
-    nc.vector.tensor_tensor(out=high_rest[:], in0=turns_high[:], in1=whole[:], op=ALU.subtract)
-    fraction = pool.tile([P, TILES, PAIRS], F32)
-    nc.vector.tensor_tensor(out=fraction[:], in0=high_rest[:], in1=turns_low[:], op=ALU.add)
-
-    minus_abs = pool.tile([P, TILES, PAIRS], F32)
-    nc.vector.scalar_tensor_tensor(
-        out=minus_abs[:], in0=fraction[:], scalar=-1.0, in1=fraction[:], op0=ALU.mult, op1=ALU.min
-    )
-    quarter_less_abs = pool.tile([P, TILES, PAIRS], F32)
-    nc.vector.tensor_scalar(
-        out=quarter_less_abs[:], in0=minus_abs[:], scalar1=0.25, scalar2=None, op0=ALU.add
-    )
-
-    turn = 2.0 * math.pi
-    nc.scalar.activation(out=table[:, :, 0, 0, :], in_=quarter_less_abs[:], func=ACT.Sin, scale=turn)
-    nc.scalar.activation(out=table[:, :, 0, 1, :], in_=fraction[:], func=ACT.Sin, scale=-turn)
-    nc.scalar.activation(out=table[:, :, 1, 0, :], in_=fraction[:], func=ACT.Sin, scale=turn)
-    nc.scalar.activation(out=table[:, :, 1, 1, :], in_=quarter_less_abs[:], func=ACT.Sin, scale=turn)
 
 
 def tile_deepseekv4attention_pb_kernel(tc, hidden, wq, out):
@@ -92,38 +44,79 @@ def tile_deepseekv4attention_pb_kernel(tc, hidden, wq, out):
     with ExitStack() as ctx:
         keep = ctx.enter_context(tc.tile_pool(name="keep", bufs=1))
         w_stage = ctx.enter_context(tc.tile_pool(name="w_stage", bufs=2))
-        h_stage = ctx.enter_context(tc.tile_pool(name="h_stage", bufs=3))
+        h_stage = ctx.enter_context(tc.tile_pool(name="h_stage", bufs=AHEAD + 2))
         work = ctx.enter_context(tc.tile_pool(name="work", bufs=3))
-        flipped_banks = ctx.enter_context(tc.psum_pool(name="flipped_banks", bufs=2))
+        flipped_banks = ctx.enter_context(tc.psum_pool(name="flipped_banks", bufs=GROUP))
         rotated_banks = ctx.enter_context(tc.psum_pool(name="rotated_banks", bufs=3))
         copied_banks = ctx.enter_context(tc.psum_pool(name="copied_banks", bufs=3))
+        ctx.enter_context(tc.manual_schedule())
 
         hidden_groups = hidden[0].rearrange("(p n x) k -> n p (x k)", n=GROUPS, x=GROUP)
         out_groups = out[0].rearrange("h (p n x) d -> n p h (x d)", n=GROUPS, x=GROUP)
+        out_tiles = out[0].rearrange("h (p i) d -> i p h d", i=TILES)
 
         h_raw = []
         for n in range(GROUPS):
             h_raw.append(keep.tile([P, GROUP * HIDDEN], BF16, name="h_raw%d" % n))
         w_raw = keep.tile([P, PASSES, PACK, HEADS * HEAD_DIM], BF16)
 
-        nc.sync.dma_start(out=h_raw[0][:], in_=hidden_groups[0])
-        for g in range(PASSES):
+        def load_wq(g):
             nc.sync.dma_start(
                 out=w_raw[:, g].rearrange("q (u e) n -> q u (e n)", u=HALVES),
                 in_=wq[g * K_PASS : (g + 1) * K_PASS, :].rearrange(
                     "(u q e) n -> q u (e n)", u=HALVES, q=P
                 ),
             )
+
+        load_wq(0)
+        nc.sync.dma_start(out=h_raw[0][:], in_=hidden_groups[0])
+        load_wq(1)
         for n in range(1, GROUPS):
             nc.sync.dma_start(out=h_raw[n][:], in_=hidden_groups[n])
 
         table = keep.tile([P, TILES, 2, 2, PAIRS], F32)
-        build_rotation_table(nc, keep, table)
 
+        warm = keep.tile([P, 1], F32)
+        nc.vector.memset(warm[:], 0.0)
+        nc.scalar.activation(out=warm[:], in_=warm[:], func=ACT.Sin)
+
+        token_int = keep.tile([P, TILES], I32)
+        nc.gpsimd.iota(token_int[:], pattern=[[1, TILES]], base=0, channel_multiplier=TILES)
         identity = keep.tile([P, P], F32)
         make_identity(nc, identity[:])
+        token = keep.tile([P, TILES], F32)
+        nc.vector.tensor_copy(out=token[:], in_=token_int[:])
 
-        def quantise_hidden(n):
+        turns = keep.tile([P, TILES, PAIRS], F32)
+        for j in range(PAIRS):
+            nc.vector.tensor_scalar(
+                out=turns[:, :, j],
+                in0=token[:],
+                scalar1=THETA ** (-j / PAIRS) / (2.0 * math.pi),
+                scalar2=None,
+                op0=ALU.mult,
+            )
+        whole = keep.tile([P, TILES, PAIRS], I32)
+        nc.vector.tensor_copy(out=whole[:], in_=turns[:])
+        fraction = keep.tile([P, TILES, PAIRS], F32)
+        nc.vector.tensor_tensor(out=fraction[:], in0=turns[:], in1=whole[:], op=ALU.subtract)
+        minus_abs = keep.tile([P, TILES, PAIRS], F32)
+        nc.vector.scalar_tensor_tensor(
+            out=minus_abs[:], in0=fraction[:], scalar=-1.0, in1=fraction[:], op0=ALU.mult, op1=ALU.min
+        )
+        quarter_less_abs = keep.tile([P, TILES, PAIRS], F32)
+        nc.vector.tensor_scalar(
+            out=quarter_less_abs[:], in0=minus_abs[:], scalar1=0.25, scalar2=None, op0=ALU.add
+        )
+        turn = 2.0 * math.pi
+        nc.scalar.activation(out=table[:, :, 0, 1, :], in_=fraction[:], func=ACT.Sin, scale=-turn)
+        nc.scalar.activation(out=table[:, :, 1, 0, :], in_=fraction[:], func=ACT.Sin, scale=turn)
+        for s in range(2):
+            nc.scalar.activation(
+                out=table[:, :, s, s, :], in_=quarter_less_abs[:], func=ACT.Sin, scale=turn
+            )
+
+        def transpose_hidden(n):
             raw_words = h_raw[n][:].bitcast(F32).rearrange("m (x w) -> m x w", x=GROUP)
             grouped = h_stage.tile([P, GROUP * PASSES * P * PACK], BF16, align_bytes=64)
             grouped_words = grouped[:].bitcast(F32).rearrange(
@@ -139,6 +132,9 @@ def tile_deepseekv4attention_pb_kernel(tc, hidden, wq, out):
                     out=grouped_words[:, x],
                     in_=flipped[:].rearrange("q (g u) m -> q g m u", u=HALVES),
                 )
+            return grouped
+
+        def quantise_hidden(grouped):
             codes = h_stage.tile([P, GROUP * PASSES * P], U32, align_bytes=64)
             scales = h_stage.tile([P, GROUP * PASSES * P], U8, align_bytes=64)
             nc.vector.quantize_mx(out=codes[:].bitcast(FP8X4), scales=scales[:], in_=grouped[:])
@@ -147,29 +143,34 @@ def tile_deepseekv4attention_pb_kernel(tc, hidden, wq, out):
         w_codes = keep.tile([P, PASSES, 2, BANK], U32, align_bytes=64)
         w_scales = keep.tile([P, PASSES, 2, BANK], U8, align_bytes=64)
 
-        def quantise_wq(g):
-            by_feature = w_raw[:, g].rearrange("q t (h s c) -> q s h c t", h=HEADS, s=2)
+        def features_of_wq(g):
+            return w_raw[:, g].rearrange("q t (h s c) -> q s h c t", h=HEADS, s=2)
 
-            rotated = w_stage.tile([P, BANK * PACK], BF16, align_bytes=64)
-            rotated_out = rotated[:].rearrange("q (r h j t) -> q r h j t", r=2, h=HEADS, t=PACK)
-            rotated_in = by_feature[:, 1].rearrange("q h (j r) t -> q r h j t", r=2)
+        def regroup_rotated(g):
+            grouped = w_stage.tile([P, BANK * PACK], BF16, align_bytes=64, tag="rotated")
+            pairs_out = grouped[:].rearrange("q (r h j t) -> q r h j t", r=2, h=HEADS, t=PACK)
+            pairs_in = features_of_wq(g)[:, 1].rearrange("q h (j r) t -> q r h j t", r=2)
             for r in range(2):
-                nc.vector.tensor_copy(out=rotated_out[:, r], in_=rotated_in[:, r])
+                nc.vector.tensor_copy(out=pairs_out[:, r], in_=pairs_in[:, r])
+            return grouped
 
-            copied = w_stage.tile([P, BANK * PACK], BF16, align_bytes=64)
-            nc.scalar.copy(
-                out=copied[:].rearrange("q (h c t) -> q h c t", h=HEADS, t=PACK),
-                in_=by_feature[:, 0],
+        def regroup_copied(g, copy):
+            grouped = w_stage.tile([P, BANK * PACK], BF16, align_bytes=64, tag="copied")
+            copy(
+                out=grouped[:].rearrange("q (h c t) -> q h c t", h=HEADS, t=PACK),
+                in_=features_of_wq(g)[:, 0],
+            )
+            return grouped
+
+        def quantise_wq(g, part, grouped):
+            nc.vector.quantize_mx(
+                out=w_codes[:, g, part, :].bitcast(FP8X4),
+                scales=w_scales[:, g, part, :],
+                in_=grouped[:],
             )
 
-            for part, grouped in ((ROTATED, rotated), (COPIED, copied)):
-                nc.vector.quantize_mx(
-                    out=w_codes[:, g, part, :].bitcast(FP8X4),
-                    scales=w_scales[:, g, part, :],
-                    in_=grouped[:],
-                )
-
         def project_and_rotate(n, codes, scales):
+            last = n == GROUPS - 1
             result = work.tile([P, HEADS, GROUP, HEAD_DIM], F32)
             for x in range(GROUP):
                 rotated_acc = rotated_banks.tile([P, BANK], F32)
@@ -198,7 +199,8 @@ def tile_deepseekv4attention_pb_kernel(tc, hidden, wq, out):
                     in1=table[:, n * GROUP + x].unsqueeze(3).to_broadcast(shape),
                     op=ALU.mult,
                 )
-                nc.gpsimd.tensor_tensor(
+                adder = nc.vector if last else nc.gpsimd
+                adder.tensor_tensor(
                     out=result[:, :, x, PLAIN:].rearrange("p h (j s) -> p h j s", s=2),
                     in0=products[:, :, 0].rearrange("p s h j -> p h j s"),
                     in1=products[:, :, 1].rearrange("p s h j -> p h j s"),
@@ -208,12 +210,27 @@ def tile_deepseekv4attention_pb_kernel(tc, hidden, wq, out):
                     out=result[:, :, x, :PLAIN],
                     in_=copied_acc[:].rearrange("p (h c) -> p h c", h=HEADS),
                 )
-            nc.sync.dma_start(out=out_groups[n], in_=result[:].rearrange("p h x d -> p h (x d)"))
+                if last:
+                    nc.sync.dma_start(out=out_tiles[n * GROUP + x], in_=result[:, :, x, :])
+            if not last:
+                nc.sync.dma_start(
+                    out=out_groups[n], in_=result[:].rearrange("p h x d -> p h (x d)")
+                )
 
-        quantised = quantise_hidden(0)
-        for g in range(PASSES):
-            quantise_wq(g)
+        h_grouped = {0: transpose_hidden(0)}
+        rotated_0 = regroup_rotated(0)
+        copied_0 = regroup_copied(0, nc.scalar.copy)
+        quantise_wq(0, ROTATED, rotated_0)
+        rotated_1 = regroup_rotated(1)
+        quantise_wq(1, ROTATED, rotated_1)
+        quantised = {0: quantise_hidden(h_grouped[0])}
+        h_grouped[1] = transpose_hidden(1)
+        copied_1 = regroup_copied(1, nc.vector.tensor_copy)
+        quantise_wq(0, COPIED, copied_0)
+        quantise_wq(1, COPIED, copied_1)
+        quantised[1] = quantise_hidden(h_grouped[1])
+
         for n in range(GROUPS):
-            following = quantise_hidden(n + 1) if n + 1 < GROUPS else None
-            project_and_rotate(n, quantised[0], quantised[1])
-            quantised = following
+            if n + AHEAD < GROUPS:
+                quantised[n + AHEAD] = quantise_hidden(transpose_hidden(n + AHEAD))
+            project_and_rotate(n, quantised[n][0], quantised[n][1])

@@ -68,10 +68,9 @@ def tile_deepseekv4attention_pb_kernel(tc, hidden, wq, out):
                 ),
             )
 
-        load_wq(0)
-        nc.sync.dma_start(out=h_raw[0][:], in_=hidden_groups[0])
-        load_wq(1)
-        for n in range(1, GROUPS):
+        for g in range(PASSES):
+            load_wq(g)
+        for n in range(GROUPS):
             nc.sync.dma_start(out=h_raw[n][:], in_=hidden_groups[n])
 
         table = keep.tile([P, TILES, 2, 2, PAIRS], F32)
@@ -169,9 +168,9 @@ def tile_deepseekv4attention_pb_kernel(tc, hidden, wq, out):
                 in_=grouped[:],
             )
 
-        def project_and_rotate(n, codes, scales):
-            last = n == GROUPS - 1
+        def project(n, codes, scales):
             result = work.tile([P, HEADS, GROUP, HEAD_DIM], F32)
+            products = work.tile([P, 2, 2, HEADS, GROUP, PAIRS], F32)
             for x in range(GROUP):
                 rotated_acc = rotated_banks.tile([P, BANK], F32)
                 copied_acc = copied_banks.tile([P, BANK], F32)
@@ -187,11 +186,9 @@ def tile_deepseekv4attention_pb_kernel(tc, hidden, wq, out):
                             start=(g == 0),
                             stop=(g == PASSES - 1),
                         )
-
                 shape = [P, 2, 2, HEADS, PAIRS]
-                products = work.tile(shape, F32)
                 nc.vector.tensor_tensor(
-                    out=products[:],
+                    out=products[:, :, :, :, x, :],
                     in0=rotated_acc[:]
                     .rearrange("p (r h j) -> p r h j", r=2, h=HEADS)
                     .unsqueeze(1)
@@ -199,38 +196,49 @@ def tile_deepseekv4attention_pb_kernel(tc, hidden, wq, out):
                     in1=table[:, n * GROUP + x].unsqueeze(3).to_broadcast(shape),
                     op=ALU.mult,
                 )
-                adder = nc.vector if last else nc.gpsimd
-                adder.tensor_tensor(
-                    out=result[:, :, x, PLAIN:].rearrange("p h (j s) -> p h j s", s=2),
-                    in0=products[:, :, 0].rearrange("p s h j -> p h j s"),
-                    in1=products[:, :, 1].rearrange("p s h j -> p h j s"),
-                    op=ALU.add,
-                )
                 nc.scalar.copy(
                     out=result[:, :, x, :PLAIN],
                     in_=copied_acc[:].rearrange("p (h c) -> p h c", h=HEADS),
                 )
-                if last:
-                    nc.sync.dma_start(out=out_tiles[n * GROUP + x], in_=result[:, :, x, :])
-            if not last:
+            return result, products
+
+        def sum_and_store(n, result, products):
+            if n < GROUPS - 1:
+                nc.gpsimd.tensor_tensor(
+                    out=result[:, :, :, PLAIN:].rearrange("p h x (j s) -> p h x j s", s=2),
+                    in0=products[:, :, 0].rearrange("p s h x j -> p h x j s"),
+                    in1=products[:, :, 1].rearrange("p s h x j -> p h x j s"),
+                    op=ALU.add,
+                )
                 nc.sync.dma_start(
                     out=out_groups[n], in_=result[:].rearrange("p h x d -> p h (x d)")
                 )
+            else:
+                for x in range(GROUP):
+                    nc.vector.tensor_tensor(
+                        out=result[:, :, x, PLAIN:].rearrange("p h (j s) -> p h j s", s=2),
+                        in0=products[:, :, 0, :, x, :].rearrange("p s h j -> p h j s"),
+                        in1=products[:, :, 1, :, x, :].rearrange("p s h j -> p h j s"),
+                        op=ALU.add,
+                    )
+                    nc.sync.dma_start(out=out_tiles[n * GROUP + x], in_=result[:, :, x, :])
 
-        h_grouped = {0: transpose_hidden(0)}
         rotated_0 = regroup_rotated(0)
         copied_0 = regroup_copied(0, nc.scalar.copy)
         quantise_wq(0, ROTATED, rotated_0)
         rotated_1 = regroup_rotated(1)
         quantise_wq(1, ROTATED, rotated_1)
-        quantised = {0: quantise_hidden(h_grouped[0])}
-        h_grouped[1] = transpose_hidden(1)
         copied_1 = regroup_copied(1, nc.vector.tensor_copy)
         quantise_wq(0, COPIED, copied_0)
         quantise_wq(1, COPIED, copied_1)
-        quantised[1] = quantise_hidden(h_grouped[1])
+        quantised = {}
+        for n in range(AHEAD):
+            quantised[n] = quantise_hidden(transpose_hidden(n))
 
         for n in range(GROUPS):
             if n + AHEAD < GROUPS:
-                quantised[n + AHEAD] = quantise_hidden(transpose_hidden(n + AHEAD))
-            project_and_rotate(n, quantised[n][0], quantised[n][1])
+                grouped = transpose_hidden(n + AHEAD)
+            result, products = project(n, quantised[n][0], quantised[n][1])
+            if n + AHEAD < GROUPS:
+                quantised[n + AHEAD] = quantise_hidden(grouped)
+            sum_and_store(n, result, products)

@@ -46,6 +46,7 @@ def tile_deepseekv4attention_pb_kernel(tc, hidden, wq, out):
         w_stage = ctx.enter_context(tc.tile_pool(name="w_stage", bufs=2))
         h_stage = ctx.enter_context(tc.tile_pool(name="h_stage", bufs=AHEAD + 2))
         work = ctx.enter_context(tc.tile_pool(name="work", bufs=3))
+        results = ctx.enter_context(tc.tile_pool(name="results", bufs=6))
         flipped_banks = ctx.enter_context(tc.psum_pool(name="flipped_banks", bufs=GROUP))
         rotated_banks = ctx.enter_context(tc.psum_pool(name="rotated_banks", bufs=3))
         copied_banks = ctx.enter_context(tc.psum_pool(name="copied_banks", bufs=3))
@@ -169,7 +170,7 @@ def tile_deepseekv4attention_pb_kernel(tc, hidden, wq, out):
             )
 
         def project(n, codes, scales):
-            result = work.tile([P, HEADS, GROUP, HEAD_DIM], F32)
+            result = results.tile([P, HEADS, GROUP, HEAD_DIM], F32)
             products = work.tile([P, 2, 2, HEADS, GROUP, PAIRS], F32)
             for x in range(GROUP):
                 rotated_acc = rotated_banks.tile([P, BANK], F32)

import math
from contextlib import ExitStack

import concourse.mybir as mybir
from concourse.masks import make_identity

F32 = mybir.dt.float32
BF16 = mybir.dt.bfloat16
I32 = mybir.dt.int32
U32 = mybir.dt.uint32
U8 = mybir.dt.uint8
FP8X4 = mybir.dt.float8_e4m3fn_x4
ALU = mybir.AluOpType
ACT = mybir.ActivationFunctionType

P = 128
TOKENS = 2048
HIDDEN = 1024
HEADS = 8
HEAD_DIM = 128
PAIRS = 32
PLAIN = HEAD_DIM - 2 * PAIRS
THETA = 10000.0

PACK = 4
HALVES = 2
K_PASS = P * PACK
PASSES = HIDDEN // K_PASS
BANK = 512

TILES = TOKENS // P
GROUP = 2
GROUPS = TILES // GROUP
AHEAD = 2

ROTATED = 0
COPIED = 1

FLOPS = 2 * TOKENS * HIDDEN * HEADS * HEAD_DIM


def tile_deepseekv4attention_pb_kernel(tc, hidden, wq, out):
    nc = tc.nc
    with ExitStack() as ctx:
        keep = ctx.enter_context(tc.tile_pool(name="keep", bufs=1))
        w_stage = ctx.enter_context(tc.tile_pool(name="w_stage", bufs=2))
        h_stage = ctx.enter_context(tc.tile_pool(name="h_stage", bufs=AHEAD + 2))
        work = ctx.enter_context(tc.tile_pool(name="work", bufs=3))
        results = ctx.enter_context(tc.tile_pool(name="results", bufs=6))
        flipped_banks = ctx.enter_context(tc.psum_pool(name="flipped_banks", bufs=GROUP))
        rotated_banks = ctx.enter_context(tc.psum_pool(name="rotated_banks", bufs=3))
        copied_banks = ctx.enter_context(tc.psum_pool(name="copied_banks", bufs=3))
        ctx.enter_context(tc.manual_schedule())

        hidden_groups = hidden[0].rearrange("(p n x) k -> n p (x k)", n=GROUPS, x=GROUP)
        out_groups = out[0].rearrange("h (p n x) d -> n p h (x d)", n=GROUPS, x=GROUP)
        out_tiles = out[0].rearrange("h (p i) d -> i p h d", i=TILES)

        h_raw = []
        for n in range(GROUPS):
            h_raw.append(keep.tile([P, GROUP * HIDDEN], BF16, name="h_raw%d" % n))
        w_raw = keep.tile([P, PASSES, PACK, HEADS * HEAD_DIM], BF16)

        def load_wq(g):
            nc.sync.dma_start(
                out=w_raw[:, g].rearrange("q (u e) n -> q u (e n)", u=HALVES),
                in_=wq[g * K_PASS : (g + 1) * K_PASS, :].rearrange(
                    "(u q e) n -> q u (e n)", u=HALVES, q=P
                ),
            )

        for g in range(PASSES):
            load_wq(g)
        for n in range(GROUPS):
            nc.sync.dma_start(out=h_raw[n][:], in_=hidden_groups[n])

        table = keep.tile([P, TILES, 2, 2, PAIRS], F32)

        warm = keep.tile([P, 1], F32)
        nc.vector.memset(warm[:], 0.0)
        nc.scalar.activation(out=warm[:], in_=warm[:], func=ACT.Sin)

        token_int = keep.tile([P, TILES], I32)
        nc.gpsimd.iota(token_int[:], pattern=[[1, TILES]], base=0, channel_multiplier=TILES)
        identity = keep.tile([P, P], F32)
        make_identity(nc, identity[:])
        token = keep.tile([P, TILES], F32)
        nc.vector.tensor_copy(out=token[:], in_=token_int[:])

        turns = keep.tile([P, TILES, PAIRS], F32)
        for j in range(PAIRS):
            nc.vector.tensor_scalar(
                out=turns[:, :, j],
                in0=token[:],
                scalar1=THETA ** (-j / PAIRS) / (2.0 * math.pi),
                scalar2=None,
                op0=ALU.mult,
            )
        whole = keep.tile([P, TILES, PAIRS], I32)
        nc.vector.tensor_copy(out=whole[:], in_=turns[:])
        fraction = keep.tile([P, TILES, PAIRS], F32)
        nc.vector.tensor_tensor(out=fraction[:], in0=turns[:], in1=whole[:], op=ALU.subtract)
        minus_abs = keep.tile([P, TILES, PAIRS], F32)
        nc.vector.scalar_tensor_tensor(
            out=minus_abs[:], in0=fraction[:], scalar=-1.0, in1=fraction[:], op0=ALU.mult, op1=ALU.min
        )
        quarter_less_abs = keep.tile([P, TILES, PAIRS], F32)
        nc.vector.tensor_scalar(
            out=quarter_less_abs[:], in0=minus_abs[:], scalar1=0.25, scalar2=None, op0=ALU.add
        )
        turn = 2.0 * math.pi
        nc.scalar.activation(out=table[:, :, 0, 1, :], in_=fraction[:], func=ACT.Sin, scale=-turn)
        nc.scalar.activation(out=table[:, :, 1, 0, :], in_=fraction[:], func=ACT.Sin, scale=turn)
        for s in range(2):
            nc.scalar.activation(
                out=table[:, :, s, s, :], in_=quarter_less_abs[:], func=ACT.Sin, scale=turn
            )

        def transpose_hidden(n):
            raw_words = h_raw[n][:].bitcast(F32).rearrange("m (x w) -> m x w", x=GROUP)
            grouped = h_stage.tile([P, GROUP * PASSES * P * PACK], BF16, align_bytes=64)
            grouped_words = grouped[:].bitcast(F32).rearrange(
                "q (x g m u) -> q x g m u", x=GROUP, g=PASSES, u=HALVES
            )
            for x in range(GROUP):
                flipped = flipped_banks.tile([P, PASSES * HALVES, P], F32)
                for c in range(PASSES * HALVES):
                    nc.tensor.transpose(
                        flipped[:, c, :], raw_words[:, x, c * P : (c + 1) * P], identity[:]
                    )
                nc.scalar.copy(
                    out=grouped_words[:, x],
                    in_=flipped[:].rearrange("q (g u) m -> q g m u", u=HALVES),
                )
            return grouped

        def quantise_hidden(grouped):
            codes = h_stage.tile([P, GROUP * PASSES * P], U32, align_bytes=64)
            scales = h_stage.tile([P, GROUP * PASSES * P], U8, align_bytes=64)
            nc.vector.quantize_mx(out=codes[:].bitcast(FP8X4), scales=scales[:], in_=grouped[:])
            return codes, scales

        w_codes = keep.tile([P, PASSES, 2, BANK], U32, align_bytes=64)
        w_scales = keep.tile([P, PASSES, 2, BANK], U8, align_bytes=64)

        def features_of_wq(g):
            return w_raw[:, g].rearrange("q t (h s c) -> q s h c t", h=HEADS, s=2)

        def regroup_rotated(g):
            grouped = w_stage.tile([P, BANK * PACK], BF16, align_bytes=64, tag="rotated")
            pairs_out = grouped[:].rearrange("q (r h j t) -> q r h j t", r=2, h=HEADS, t=PACK)
            pairs_in = features_of_wq(g)[:, 1].rearrange("q h (j r) t -> q r h j t", r=2)
            for r in range(2):
                nc.vector.tensor_copy(out=pairs_out[:, r], in_=pairs_in[:, r])
            return grouped

        def regroup_copied(g, copy):
            grouped = w_stage.tile([P, BANK * PACK], BF16, align_bytes=64, tag="copied")
            copy(
                out=grouped[:].rearrange("q (h c t) -> q h c t", h=HEADS, t=PACK),
                in_=features_of_wq(g)[:, 0],
            )
            return grouped

        def quantise_wq(g, part, grouped):
            nc.vector.quantize_mx(
                out=w_codes[:, g, part, :].bitcast(FP8X4),
                scales=w_scales[:, g, part, :],
                in_=grouped[:],
            )

        def project(n, codes, scales):
            result = results.tile([P, HEADS, GROUP, HEAD_DIM], F32)
            products = work.tile([P, 2, 2, HEADS, GROUP, PAIRS], F32)
            for x in range(GROUP):
                rotated_acc = rotated_banks.tile([P, BANK], F32)
                copied_acc = copied_banks.tile([P, BANK], F32)
                for part, acc in ((ROTATED, rotated_acc), (COPIED, copied_acc)):
                    for g in range(PASSES):
                        tokens = slice((x * PASSES + g) * P, (x * PASSES + g + 1) * P)
                        nc.tensor.matmul_mx(
                            out=acc[:],
                            lhsT=codes[:, tokens].bitcast(FP8X4),
                            lhsT_scale=scales[:, tokens],
                            rhs=w_codes[:, g, part, :].bitcast(FP8X4),
                            rhs_scale=w_scales[:, g, part, :],
                            start=(g == 0),
                            stop=(g == PASSES - 1),
                        )
                shape = [P, 2, 2, HEADS, PAIRS]
                nc.vector.tensor_tensor(
                    out=products[:, :, :, :, x, :],
                    in0=rotated_acc[:]
                    .rearrange("p (r h j) -> p r h j", r=2, h=HEADS)
                    .unsqueeze(1)
                    .to_broadcast(shape),
                    in1=table[:, n * GROUP + x].unsqueeze(3).to_broadcast(shape),
                    op=ALU.mult,
                )
                nc.scalar.copy(
                    out=result[:, :, x, :PLAIN],
                    in_=copied_acc[:].rearrange("p (h c) -> p h c", h=HEADS),
                )
            return result, products

        def sum_and_store(n, result, products):
            if n < GROUPS - 1:
                nc.gpsimd.tensor_tensor(
                    out=result[:, :, :, PLAIN:].rearrange("p h x (j s) -> p h x j s", s=2),
                    in0=products[:, :, 0].rearrange("p s h x j -> p h x j s"),
                    in1=products[:, :, 1].rearrange("p s h x j -> p h x j s"),
                    op=ALU.add,
                )
                nc.sync.dma_start(
                    out=out_groups[n], in_=result[:].rearrange("p h x d -> p h (x d)")
                )
            else:
                for x in range(GROUP):
                    nc.vector.tensor_tensor(
                        out=result[:, :, x, PLAIN:].rearrange("p h (j s) -> p h j s", s=2),
                        in0=products[:, :, 0, :, x, :].rearrange("p s h j -> p h j s"),
                        in1=products[:, :, 1, :, x, :].rearrange("p s h j -> p h j s"),
                        op=ALU.add,
                    )
                    nc.sync.dma_start(out=out_tiles[n * GROUP + x], in_=result[:, :, x, :])

        rotated_0 = regroup_rotated(0)
        copied_0 = regroup_copied(0, nc.scalar.copy)
        quantise_wq(0, ROTATED, rotated_0)
        rotated_1 = regroup_rotated(1)
        quantise_wq(1, ROTATED, rotated_1)
        copied_1 = regroup_copied(1, nc.vector.tensor_copy)
        quantise_wq(0, COPIED, copied_0)
        quantise_wq(1, COPIED, copied_1)
        quantised = {}
        for n in range(AHEAD):
            quantised[n] = quantise_hidden(transpose_hidden(n))

        for n in range(GROUPS):
            if n + AHEAD < GROUPS:
                grouped = transpose_hidden(n + AHEAD)
            result, products = project(n, quantised[n][0], quantised[n][1])
            if n + AHEAD < GROUPS:
                quantised[n + AHEAD] = quantise_hidden(grouped)
            sum_and_store(n, result, products)
